import numpy as np
import ml_dtypes

BF16 = ml_dtypes.bfloat16


def bf(x):
    return np.asarray(x, np.float32).astype(BF16)


def f32(x):
    return np.asarray(x, np.float32)


def f64(x):
    return np.asarray(x).astype(np.float64)


def striped(idx):
    return np.tile(idx.reshape(-1, 16).T, (8, 1))


D, S, F, K, R, N = 128, 1024, 512, 128, 128, 2048


def relu(v):
    return np.maximum(v, 0.0)


def setup_inputs():
    return {"table": bf(np.random.standard_normal((D, S))), "w0": bf(np.random.standard_normal((D, F)) / np.sqrt(D)), "b0": f32(0.1 * np.random.standard_normal((F, 1))), "w1": bf(np.random.standard_normal((F, F)) * np.sqrt(2.0 / F)), "b1": f32(0.1 * np.random.standard_normal((F, 1))), "w_head": bf(np.random.standard_normal((F, K)) * np.sqrt(2.0 / F)), "b_head": f32(0.1 * np.random.standard_normal((K, 1))), "offs": striped(np.random.permutation(np.tile(np.arange(S), 2))[:N])}


def reference(table, w0, b0, w1, b1, w_head, b_head, offs):
    idx = offs[:16].T.reshape(-1)
    h0 = relu(f64(w0).T @ f64(table)[:, idx] + f64(b0))
    h0r = np.roll(h0, -R, axis=0)
    h1 = relu(f64(w1).T @ h0r + f64(b1))
    h1r = np.roll(h1, R, axis=0)
    return f64(w_head).T @ h1r + f64(b_head)

@@ -1,0 +1,102 @@
+import concourse.mybir as mybir
+
+BF16, F32, U16 = mybir.dt.bfloat16, mybir.dt.float32, mybir.dt.uint16
+ADD, MAX = mybir.AluOpType.add, mybir.AluOpType.max
+RELU, IDENTITY = mybir.ActivationFunctionType.Relu, mybir.ActivationFunctionType.Identity
+
+P = 128
+STORE = 1024
+BATCH = 2048
+HIDDEN = 512
+BLOCKS = HIDDEN // P
+PIECE = 512
+PIECES = BATCH // PIECE
+PER_COLUMN = 16
+
+FLOPS = 2 * BATCH * (P * HIDDEN + HIDDEN * HIDDEN + HIDDEN * P)
+
+
+def add_bias(nc, turn, result, bank, bias, relu):
+    if turn % 2 == 0:
+        nc.scalar.activation(result, bank, RELU if relu else IDENTITY, bias=bias)
+    elif relu:
+        nc.vector.tensor_scalar(result, bank, bias, 0.0, ADD, MAX)
+    else:
+        nc.vector.tensor_scalar_add(result, bank, bias)
+
+
+def tile_capsuleneuralnetwork_kernel(tc, table, w0, b0, w1, b1, w_head, b_head, offs, out):
+    nc = tc.nc
+    with (
+        tc.tile_pool(name="held", bufs=1) as held,
+        tc.tile_pool(name="leaving", bufs=2) as leaving,
+        tc.psum_pool(name="banks", bufs=8) as banks,
+    ):
+        offsets = held.tile([P, BATCH // PER_COLUMN], U16, name="offsets")
+        nc.sync.dma_start(offsets[:], offs)
+        store = held.tile([P, STORE], BF16, name="store")
+        nc.sync.dma_start(store[:], table)
+        w0_sb = held.tile([P, HIDDEN], BF16, name="w0_sb")
+        nc.scalar.dma_start(w0_sb[:], w0)
+
+        w1_sb = held.tile([P, BLOCKS, HIDDEN], BF16, name="w1_sb")
+        w_head_sb = held.tile([P, BLOCKS, P], BF16, name="w_head_sb")
+        b0_sb = held.tile([P, BLOCKS], F32, name="b0_sb")
+        b1_sb = held.tile([P, BLOCKS], F32, name="b1_sb")
+        b_head_sb = held.tile([P, 1], F32, name="b_head_sb")
+        with nc.allow_non_contiguous_dma(reason="a bias has one float32 for each partition and block"):
+            nc.scalar.dma_start(b0_sb[:], b0.rearrange("(block p) one -> p (block one)", p=P))
+            nc.sync.dma_start(w1_sb[:], w1.rearrange("(block p) m -> p block m", p=P))
+            nc.sync.dma_start(b1_sb[:], b1.rearrange("(block p) one -> p (block one)", p=P))
+            nc.sync.dma_start(w_head_sb[:], w_head.rearrange("(block p) q -> p block q", p=P))
+            nc.sync.dma_start(b_head_sb[:], b_head)
+
+        h0 = held.tile([P, BLOCKS, BATCH], BF16, name="h0")
+        h1 = held.tile([P, BLOCKS, BATCH], BF16, name="h1")
+        turn = 0
+
+        for piece in range(PIECES):
+            samples = slice(piece * PIECE, (piece + 1) * PIECE)
+            entries = slice(piece * PIECE // PER_COLUMN, (piece + 1) * PIECE // PER_COLUMN)
+            for block in range(BLOCKS):
+                bank = banks.tile([P, PIECE], F32, name="bank")
+                nc.tensor.matmul(
+                    bank[:],
+                    w0_sb[:, block * P : (block + 1) * P],
+                    store[:].indirect(offsets[:, entries]),
+                    start=True,
+                    stop=True,
+                )
+                add_bias(nc, turn, h0[:, block, samples], bank[:], b0_sb[:, block : block + 1], relu=True)
+                turn += 1
+
+        for piece in range(PIECES):
+            samples = slice(piece * PIECE, (piece + 1) * PIECE)
+            for block in range(BLOCKS):
+                bank = banks.tile([P, PIECE], F32, name="bank")
+                for k in range(BLOCKS):
+                    nc.tensor.matmul(
+                        bank[:],
+                        w1_sb[:, k, block * P : (block + 1) * P],
+                        h0[:, (k + 1) % BLOCKS, samples],
+                        start=(k == 0),
+                        stop=(k == BLOCKS - 1),
+                    )
+                add_bias(nc, turn, h1[:, block, samples], bank[:], b1_sb[:, block : block + 1], relu=True)
+                turn += 1
+
+        for piece in range(PIECES):
+            samples = slice(piece * PIECE, (piece + 1) * PIECE)
+            bank = banks.tile([P, PIECE], F32, name="bank")
+            for k in range(BLOCKS):
+                nc.tensor.matmul(
+                    bank[:],
+                    w_head_sb[:, k, :],
+                    h1[:, (k - 1) % BLOCKS, samples],
+                    start=(k == 0),
+                    stop=(k == BLOCKS - 1),
+                )
+            result = leaving.tile([P, PIECE], F32, name="result")
+            add_bias(nc, turn, result[:], bank[:], b_head_sb[:, 0:1], relu=False)
+            turn += 1
+            nc.sync.dma_start(out[:, samples], result[:])

@@ -12,6 +12,7 @@ BLOCKS = HIDDEN // P
 PIECE = 512
 PIECES = BATCH // PIECE
 PER_COLUMN = 16
+WARM_UP = 6
 
 FLOPS = 2 * BATCH * (P * HIDDEN + HIDDEN * HIDDEN + HIDDEN * P)
 
@@ -30,7 +31,8 @@ def tile_capsuleneuralnetwork_kernel(tc, table, w0, b0, w1, b1, w_head, b_head, 
     with (
         tc.tile_pool(name="held", bufs=1) as held,
         tc.tile_pool(name="leaving", bufs=2) as leaving,
-        tc.psum_pool(name="banks", bufs=8) as banks,
+        tc.psum_pool(name="idle", bufs=1) as idle,
+        tc.psum_pool(name="banks", bufs=7) as banks,
     ):
         offsets = held.tile([P, BATCH // PER_COLUMN], U16, name="offsets")
         nc.sync.dma_start(offsets[:], offs)
@@ -50,6 +52,12 @@ def tile_capsuleneuralnetwork_kernel(tc, table, w0, b0, w1, b1, w_head, b_head, 
             nc.sync.dma_start(b1_sb[:], b1.rearrange("(block p) one -> p (block one)", p=P))
             nc.sync.dma_start(w_head_sb[:], w_head.rearrange("(block p) q -> p block q", p=P))
             nc.sync.dma_start(b_head_sb[:], b_head)
+
+        zeros = held.tile([P, PIECE], BF16, name="zeros")
+        nc.vector.memset(zeros[:], 0.0)
+        unread = idle.tile([P, PIECE], F32, name="unread")
+        for repeat in range(WARM_UP):
+            nc.tensor.matmul(unread[:], zeros[:, 0:P], zeros[:], start=True, stop=True)
 
         h0 = held.tile([P, BLOCKS, BATCH], BF16, name="h0")
         h1 = held.tile([P, BLOCKS, BATCH], BF16, name="h1")

@@ -12,7 +12,6 @@ BLOCKS = HIDDEN // P
 PIECE = 512
 PIECES = BATCH // PIECE
 PER_COLUMN = 16
-WARM_UP = 6
 
 FLOPS = 2 * BATCH * (P * HIDDEN + HIDDEN * HIDDEN + HIDDEN * P)
 
@@ -30,9 +29,7 @@ def tile_capsuleneuralnetwork_kernel(tc, table, w0, b0, w1, b1, w_head, b_head, 
     nc = tc.nc
     with (
         tc.tile_pool(name="held", bufs=1) as held,
-        tc.tile_pool(name="leaving", bufs=2) as leaving,
-        tc.psum_pool(name="idle", bufs=1) as idle,
-        tc.psum_pool(name="banks", bufs=7) as banks,
+        tc.psum_pool(name="banks", bufs=8) as banks,
     ):
         offsets = held.tile([P, BATCH // PER_COLUMN], U16, name="offsets")
         nc.sync.dma_start(offsets[:], offs)
@@ -53,14 +50,9 @@ def tile_capsuleneuralnetwork_kernel(tc, table, w0, b0, w1, b1, w_head, b_head, 
             nc.sync.dma_start(w_head_sb[:], w_head.rearrange("(block p) q -> p block q", p=P))
             nc.sync.dma_start(b_head_sb[:], b_head)
 
-        zeros = held.tile([P, PIECE], BF16, name="zeros")
-        nc.vector.memset(zeros[:], 0.0)
-        unread = idle.tile([P, PIECE], F32, name="unread")
-        for repeat in range(WARM_UP):
-            nc.tensor.matmul(unread[:], zeros[:, 0:P], zeros[:], start=True, stop=True)
-
         h0 = held.tile([P, BLOCKS, BATCH], BF16, name="h0")
         h1 = held.tile([P, BLOCKS, BATCH], BF16, name="h1")
+        result = held.tile([P, BATCH], F32, name="result")
         turn = 0
 
         for piece in range(PIECES):
@@ -104,7 +96,6 @@ def tile_capsuleneuralnetwork_kernel(tc, table, w0, b0, w1, b1, w_head, b_head, 
                     start=(k == 0),
                     stop=(k == BLOCKS - 1),
                 )
-            result = leaving.tile([P, PIECE], F32, name="result")
-            add_bias(nc, turn, result[:], bank[:], b_head_sb[:, 0:1], relu=False)
+            add_bias(nc, turn, result[:, samples], bank[:], b_head_sb[:, 0:1], relu=False)
             turn += 1
-            nc.sync.dma_start(out[:, samples], result[:])
+            nc.sync.dma_start(out[:, samples], result[:, samples])

@@ -11,6 +11,7 @@ HIDDEN = 512
 BLOCKS = HIDDEN // P
 PIECE = 512
 PIECES = BATCH // PIECE
+LAST_PIECE = 256
 PER_COLUMN = 16
 
 FLOPS = 2 * BATCH * (P * HIDDEN + HIDDEN * HIDDEN + HIDDEN * P)
@@ -85,9 +86,9 @@ def tile_capsuleneuralnetwork_kernel(tc, table, w0, b0, w1, b1, w_head, b_head, 
                 add_bias(nc, turn, h1[:, block, samples], bank[:], b1_sb[:, block : block + 1], relu=True)
                 turn += 1
 
-        for piece in range(PIECES):
-            samples = slice(piece * PIECE, (piece + 1) * PIECE)
-            bank = banks.tile([P, PIECE], F32, name="bank")
+        for piece in range(BATCH // LAST_PIECE):
+            samples = slice(piece * LAST_PIECE, (piece + 1) * LAST_PIECE)
+            bank = banks.tile([P, LAST_PIECE], F32, name="bank")
             for k in range(BLOCKS):
                 nc.tensor.matmul(
                     bank[:],

@@ -86,17 +86,22 @@ def tile_capsuleneuralnetwork_kernel(tc, table, w0, b0, w1, b1, w_head, b_head, 
                 add_bias(nc, turn, h1[:, block, samples], bank[:], b1_sb[:, block : block + 1], relu=True)
                 turn += 1
 
-        for piece in range(BATCH // LAST_PIECE):
-            samples = slice(piece * LAST_PIECE, (piece + 1) * LAST_PIECE)
-            bank = banks.tile([P, LAST_PIECE], F32, name="bank")
-            for k in range(BLOCKS):
-                nc.tensor.matmul(
-                    bank[:],
-                    w_head_sb[:, k, :],
-                    h1[:, (k - 1) % BLOCKS, samples],
-                    start=(k == 0),
-                    stop=(k == BLOCKS - 1),
-                )
-            add_bias(nc, turn, result[:, samples], bank[:], b_head_sb[:, 0:1], relu=False)
-            turn += 1
-            nc.sync.dma_start(out[:, samples], result[:, samples])
+        read_out_pieces = BATCH // LAST_PIECE
+        for piece in range(read_out_pieces):
+            halves = 2 if piece == read_out_pieces - 1 else 1
+            width = LAST_PIECE // halves
+            for half in range(halves):
+                first = piece * LAST_PIECE + half * width
+                samples = slice(first, first + width)
+                bank = banks.tile([P, width], F32, name="bank")
+                for k in range(BLOCKS):
+                    nc.tensor.matmul(
+                        bank[:],
+                        w_head_sb[:, k, :],
+                        h1[:, (k - 1) % BLOCKS, samples],
+                        start=(k == 0),
+                        stop=(k == BLOCKS - 1),
+                    )
+                add_bias(nc, piece + 1 + half, result[:, samples], bank[:], b_head_sb[:, 0:1], relu=False)
+            whole = slice(piece * LAST_PIECE, (piece + 1) * LAST_PIECE)
+            nc.sync.dma_start(out[:, whole], result[:, whole])

@@ -11,7 +11,8 @@ HIDDEN = 512
 BLOCKS = HIDDEN // P
 PIECE = 512
 PIECES = BATCH // PIECE
-LAST_PIECE = 256
+HALF_HIDDEN = HIDDEN // 2
+READ_OUT_PIECES = [512] + [256] * 6
 PER_COLUMN = 16
 
 FLOPS = 2 * BATCH * (P * HIDDEN + HIDDEN * HIDDEN + HIDDEN * P)
@@ -37,7 +38,8 @@ def tile_capsuleneuralnetwork_kernel(tc, table, w0, b0, w1, b1, w_head, b_head, 
         store = held.tile([P, STORE], BF16, name="store")
         nc.sync.dma_start(store[:], table)
         w0_sb = held.tile([P, HIDDEN], BF16, name="w0_sb")
-        nc.scalar.dma_start(w0_sb[:], w0)
+        nc.scalar.dma_start(w0_sb[:, :HALF_HIDDEN], w0[:, :HALF_HIDDEN])
+        nc.sync.dma_start(w0_sb[:, HALF_HIDDEN:], w0[:, HALF_HIDDEN:])
 
         w1_sb = held.tile([P, BLOCKS, HIDDEN], BF16, name="w1_sb")
         w_head_sb = held.tile([P, BLOCKS, P], BF16, name="w_head_sb")
@@ -86,12 +88,12 @@ def tile_capsuleneuralnetwork_kernel(tc, table, w0, b0, w1, b1, w_head, b_head, 
                 add_bias(nc, turn, h1[:, block, samples], bank[:], b1_sb[:, block : block + 1], relu=True)
                 turn += 1
 
-        read_out_pieces = BATCH // LAST_PIECE
-        for piece in range(read_out_pieces):
-            halves = 2 if piece == read_out_pieces - 1 else 1
-            width = LAST_PIECE // halves
+        begin = 0
+        for piece, samples_in_piece in enumerate(READ_OUT_PIECES):
+            halves = 2 if piece == len(READ_OUT_PIECES) - 1 else 1
+            width = samples_in_piece // halves
             for half in range(halves):
-                first = piece * LAST_PIECE + half * width
+                first = begin + half * width
                 samples = slice(first, first + width)
                 bank = banks.tile([P, width], F32, name="bank")
                 for k in range(BLOCKS):
@@ -102,6 +104,7 @@ def tile_capsuleneuralnetwork_kernel(tc, table, w0, b0, w1, b1, w_head, b_head, 
                         start=(k == 0),
                         stop=(k == BLOCKS - 1),
                     )
-                add_bias(nc, piece + 1 + half, result[:, samples], bank[:], b_head_sb[:, 0:1], relu=False)
-            whole = slice(piece * LAST_PIECE, (piece + 1) * LAST_PIECE)
+                add_bias(nc, piece + half, result[:, samples], bank[:], b_head_sb[:, 0:1], relu=False)
+            whole = slice(begin, begin + samples_in_piece)
             nc.sync.dma_start(out[:, whole], result[:, whole])
+            begin += samples_in_piece

@@ -58,10 +58,10 @@ def tile_capsuleneuralnetwork_kernel(tc, table, w0, b0, w1, b1, w_head, b_head, 
         result = held.tile([P, BATCH], F32, name="result")
         turn = 0
 
-        for piece in range(PIECES):
-            samples = slice(piece * PIECE, (piece + 1) * PIECE)
-            entries = slice(piece * PIECE // PER_COLUMN, (piece + 1) * PIECE // PER_COLUMN)
-            for block in range(BLOCKS):
+        for block in range(BLOCKS):
+            for piece in range(PIECES):
+                samples = slice(piece * PIECE, (piece + 1) * PIECE)
+                entries = slice(piece * PIECE // PER_COLUMN, (piece + 1) * PIECE // PER_COLUMN)
                 bank = banks.tile([P, PIECE], F32, name="bank")
                 nc.tensor.matmul(
                     bank[:],

@@ -11,8 +11,8 @@ HIDDEN = 512
 BLOCKS = HIDDEN // P
 PIECE = 512
 PIECES = BATCH // PIECE
-HALF_HIDDEN = HIDDEN // 2
-READ_OUT_PIECES = [512] + [256] * 6
+LAST_TO_SCALAR = 3 / 4
+READ_OUT_PIECES = [512] * 2 + [256] * 4
 PER_COLUMN = 16
 
 FLOPS = 2 * BATCH * (P * HIDDEN + HIDDEN * HIDDEN + HIDDEN * P)
@@ -38,16 +38,18 @@ def tile_capsuleneuralnetwork_kernel(tc, table, w0, b0, w1, b1, w_head, b_head, 
         store = held.tile([P, STORE], BF16, name="store")
         nc.sync.dma_start(store[:], table)
         w0_sb = held.tile([P, HIDDEN], BF16, name="w0_sb")
-        nc.scalar.dma_start(w0_sb[:, :HALF_HIDDEN], w0[:, :HALF_HIDDEN])
-        nc.sync.dma_start(w0_sb[:, HALF_HIDDEN:], w0[:, HALF_HIDDEN:])
+        nc.scalar.dma_start(w0_sb[:, :P], w0[:, :P])
+        nc.sync.dma_start(w0_sb[:, P:], w0[:, P:])
 
         w1_sb = held.tile([P, BLOCKS, HIDDEN], BF16, name="w1_sb")
         w_head_sb = held.tile([P, BLOCKS, P], BF16, name="w_head_sb")
-        b0_sb = held.tile([P, BLOCKS], F32, name="b0_sb")
+        b0_first = held.tile([P, 1], F32, name="b0_first")
+        b0_rest = held.tile([P, BLOCKS - 1], F32, name="b0_rest")
         b1_sb = held.tile([P, BLOCKS], F32, name="b1_sb")
         b_head_sb = held.tile([P, 1], F32, name="b_head_sb")
         with nc.allow_non_contiguous_dma(reason="a bias has one float32 for each partition and block"):
-            nc.scalar.dma_start(b0_sb[:], b0.rearrange("(block p) one -> p (block one)", p=P))
+            nc.scalar.dma_start(b0_first[:], b0[:P, :])
+            nc.sync.dma_start(b0_rest[:], b0[P:, :].rearrange("(block p) one -> p (block one)", p=P))
             nc.sync.dma_start(w1_sb[:], w1.rearrange("(block p) m -> p block m", p=P))
             nc.sync.dma_start(b1_sb[:], b1.rearrange("(block p) one -> p (block one)", p=P))
             nc.sync.dma_start(w_head_sb[:], w_head.rearrange("(block p) q -> p block q", p=P))
@@ -59,6 +61,7 @@ def tile_capsuleneuralnetwork_kernel(tc, table, w0, b0, w1, b1, w_head, b_head, 
         turn = 0
 
         for block in range(BLOCKS):
+            bias = b0_first[:] if block == 0 else b0_rest[:, block - 1 : block]
             for piece in range(PIECES):
                 samples = slice(piece * PIECE, (piece + 1) * PIECE)
                 entries = slice(piece * PIECE // PER_COLUMN, (piece + 1) * PIECE // PER_COLUMN)
@@ -70,7 +73,7 @@ def tile_capsuleneuralnetwork_kernel(tc, table, w0, b0, w1, b1, w_head, b_head, 
                     start=True,
                     stop=True,
                 )
-                add_bias(nc, turn, h0[:, block, samples], bank[:], b0_sb[:, block : block + 1], relu=True)
+                add_bias(nc, turn, h0[:, block, samples], bank[:], bias, relu=True)
                 turn += 1
 
         for piece in range(PIECES):
@@ -90,12 +93,13 @@ def tile_capsuleneuralnetwork_kernel(tc, table, w0, b0, w1, b1, w_head, b_head, 
 
         begin = 0
         for piece, samples_in_piece in enumerate(READ_OUT_PIECES):
-            halves = 2 if piece == len(READ_OUT_PIECES) - 1 else 1
-            width = samples_in_piece // halves
-            for half in range(halves):
-                first = begin + half * width
-                samples = slice(first, first + width)
-                bank = banks.tile([P, width], F32, name="bank")
+            end = begin + samples_in_piece
+            cuts = [begin, end]
+            if piece == len(READ_OUT_PIECES) - 1:
+                cuts = [begin, begin + int(samples_in_piece * LAST_TO_SCALAR), end]
+            for part in range(len(cuts) - 1):
+                samples = slice(cuts[part], cuts[part + 1])
+                bank = banks.tile([P, cuts[part + 1] - cuts[part]], F32, name="bank")
                 for k in range(BLOCKS):
                     nc.tensor.matmul(
                         bank[:],
@@ -104,7 +108,6 @@ def tile_capsuleneuralnetwork_kernel(tc, table, w0, b0, w1, b1, w_head, b_head, 
                         start=(k == 0),
                         stop=(k == BLOCKS - 1),
                     )
-                add_bias(nc, piece + half, result[:, samples], bank[:], b_head_sb[:, 0:1], relu=False)
-            whole = slice(begin, begin + samples_in_piece)
-            nc.sync.dma_start(out[:, whole], result[:, whole])
-            begin += samples_in_piece
+                add_bias(nc, piece + 1 + part, result[:, samples], bank[:], b_head_sb[:, 0:1], relu=False)
+            nc.sync.dma_start(out[:, begin:end], result[:, begin:end])
+            begin = end

import concourse.mybir as mybir

BF16, F32, U16 = mybir.dt.bfloat16, mybir.dt.float32, mybir.dt.uint16
ADD, MAX = mybir.AluOpType.add, mybir.AluOpType.max
RELU, IDENTITY = mybir.ActivationFunctionType.Relu, mybir.ActivationFunctionType.Identity

P = 128
STORE = 1024
BATCH = 2048
HIDDEN = 512
BLOCKS = HIDDEN // P
PIECE = 512
PIECES = BATCH // PIECE
LAST_TO_SCALAR = 3 / 4
READ_OUT_PIECES = [512] * 2 + [256] * 4
PER_COLUMN = 16

FLOPS = 2 * BATCH * (P * HIDDEN + HIDDEN * HIDDEN + HIDDEN * P)


def add_bias(nc, turn, result, bank, bias, relu):
    if turn % 2 == 0:
        nc.scalar.activation(result, bank, RELU if relu else IDENTITY, bias=bias)
    elif relu:
        nc.vector.tensor_scalar(result, bank, bias, 0.0, ADD, MAX)
    else:
        nc.vector.tensor_scalar_add(result, bank, bias)


def tile_capsuleneuralnetwork_kernel(tc, table, w0, b0, w1, b1, w_head, b_head, offs, out):
    nc = tc.nc
    with (
        tc.tile_pool(name="held", bufs=1) as held,
        tc.psum_pool(name="banks", bufs=8) as banks,
    ):
        offsets = held.tile([P, BATCH // PER_COLUMN], U16, name="offsets")
        nc.sync.dma_start(offsets[:], offs)
        store = held.tile([P, STORE], BF16, name="store")
        nc.sync.dma_start(store[:], table)
        w0_sb = held.tile([P, HIDDEN], BF16, name="w0_sb")
        nc.scalar.dma_start(w0_sb[:, :P], w0[:, :P])
        nc.sync.dma_start(w0_sb[:, P:], w0[:, P:])

        w1_sb = held.tile([P, BLOCKS, HIDDEN], BF16, name="w1_sb")
        w_head_sb = held.tile([P, BLOCKS, P], BF16, name="w_head_sb")
        b0_first = held.tile([P, 1], F32, name="b0_first")
        b0_rest = held.tile([P, BLOCKS - 1], F32, name="b0_rest")
        b1_sb = held.tile([P, BLOCKS], F32, name="b1_sb")
        b_head_sb = held.tile([P, 1], F32, name="b_head_sb")
        with nc.allow_non_contiguous_dma(reason="a bias has one float32 for each partition and block"):
            nc.scalar.dma_start(b0_first[:], b0[:P, :])
            nc.sync.dma_start(b0_rest[:], b0[P:, :].rearrange("(block p) one -> p (block one)", p=P))
            nc.sync.dma_start(w1_sb[:], w1.rearrange("(block p) m -> p block m", p=P))
            nc.sync.dma_start(b1_sb[:], b1.rearrange("(block p) one -> p (block one)", p=P))
            nc.sync.dma_start(w_head_sb[:], w_head.rearrange("(block p) q -> p block q", p=P))
            nc.sync.dma_start(b_head_sb[:], b_head)

        h0 = held.tile([P, BLOCKS, BATCH], BF16, name="h0")
        h1 = held.tile([P, BLOCKS, BATCH], BF16, name="h1")
        result = held.tile([P, BATCH], F32, name="result")
        turn = 0

        for block in range(BLOCKS):
            bias = b0_first[:] if block == 0 else b0_rest[:, block - 1 : block]
            for piece in range(PIECES):
                samples = slice(piece * PIECE, (piece + 1) * PIECE)
                entries = slice(piece * PIECE // PER_COLUMN, (piece + 1) * PIECE // PER_COLUMN)
                bank = banks.tile([P, PIECE], F32, name="bank")
                nc.tensor.matmul(
                    bank[:],
                    w0_sb[:, block * P : (block + 1) * P],
                    store[:].indirect(offsets[:, entries]),
                    start=True,
                    stop=True,
                )
                add_bias(nc, turn, h0[:, block, samples], bank[:], bias, relu=True)
                turn += 1

        for piece in range(PIECES):
            samples = slice(piece * PIECE, (piece + 1) * PIECE)
            for block in range(BLOCKS):
                bank = banks.tile([P, PIECE], F32, name="bank")
                for k in range(BLOCKS):
                    nc.tensor.matmul(
                        bank[:],
                        w1_sb[:, k, block * P : (block + 1) * P],
                        h0[:, (k + 1) % BLOCKS, samples],
                        start=(k == 0),
                        stop=(k == BLOCKS - 1),
                    )
                add_bias(nc, turn, h1[:, block, samples], bank[:], b1_sb[:, block : block + 1], relu=True)
                turn += 1

        begin = 0
        for piece, samples_in_piece in enumerate(READ_OUT_PIECES):
            end = begin + samples_in_piece
            cuts = [begin, end]
            if piece == len(READ_OUT_PIECES) - 1:
                cuts = [begin, begin + int(samples_in_piece * LAST_TO_SCALAR), end]
            for part in range(len(cuts) - 1):
                samples = slice(cuts[part], cuts[part + 1])
                bank = banks.tile([P, cuts[part + 1] - cuts[part]], F32, name="bank")
                for k in range(BLOCKS):
                    nc.tensor.matmul(
                        bank[:],
                        w_head_sb[:, k, :],
                        h1[:, (k - 1) % BLOCKS, samples],
                        start=(k == 0),
                        stop=(k == BLOCKS - 1),
                    )
                add_bias(nc, piece + 1 + part, result[:, samples], bank[:], b_head_sb[:, 0:1], relu=False)
            nc.sync.dma_start(out[:, begin:end], result[:, begin:end])
            begin = end
